import numpy as np
import ml_dtypes


def mxq(x, axis, fmt="e4m3"):
    dtype, down = {"e4m3": (ml_dtypes.float8_e4m3fn, 7), "e5m2": (ml_dtypes.float8_e5m2, 14)}[fmt]
    v = np.moveaxis(np.asarray(x, np.float32).astype(ml_dtypes.bfloat16).astype(np.float64), axis, -1)
    blocks = v.reshape(v.shape[:-1] + (-1, 32))
    amax = np.abs(blocks).max(-1, keepdims=True)
    byte = np.maximum(np.where(amax > 0, np.frexp(amax)[1] - 1 + 127, 0) - down, 1)
    scale = np.exp2(byte - 127.0)
    codes = (blocks / scale).astype(np.float32).astype(dtype).astype(np.float64)
    return np.moveaxis((codes * scale).reshape(v.shape), -1, axis)


WIDE = False


def mx_kscale(k):
    if not WIDE:
        return np.ones(k)
    levels = np.array([18, -18])
    if k % 512:
        return np.exp2(np.random.permutation(np.resize(levels, k // 32))).repeat(32)
    a = np.empty((k // 512, 16))
    for p in range(k // 512):
        a[p, :8] = np.random.permutation(np.resize(levels, 8))
        for g in range(8):
            far = levels[np.abs(levels - a[p, g]) >= 10]
            a[p, g + 8] = far[np.random.randint(len(far))]
    return np.exp2(a.ravel()).repeat(32)


BF16 = ml_dtypes.bfloat16


def bf(x):
    return np.asarray(x, np.float32).astype(BF16)


def f64(x):
    return np.asarray(x).astype(np.float64)


B, C, N, T, Q = 1, 128, 1024, 8, 4


def setup_inputs():
    s = mx_kscale(C * T).reshape(C, 1, T)
    u = mx_kscale(N)
    a = 2.0 / np.sqrt(N)
    return {"x": bf(np.random.standard_normal((B, C, N, T)) * s),
            "Ar": bf(np.random.uniform(0.0, 1.0, (N, N)) * a / u[:, None]),
            "Ai": bf(np.random.uniform(0.0, 1.0, (N, N)) * a / u[:, None]),
            "Aj": bf(np.random.uniform(0.0, 1.0, (N, N)) * a / u[:, None]),
            "Ak": bf(np.random.uniform(0.0, 1.0, (N, N)) * a / u[:, None]),
            "grad_out": bf(np.random.standard_normal((B, C, N, T)) * np.exp2(np.random.randint(-6, 1, (B, 1, N, T))) / s * u[:, None])}


def reference(x, Ar, Ai, Aj, Ak, grad_out):
    g = f64(grad_out)[0].transpose(1, 0, 2).reshape(N, C * T)
    xn = f64(x)[0].transpose(1, 0, 2).reshape(N, C * T)
    gq = mxq(g, 0, "e5m2")
    Pr = mxq(f64(Ar), 0, "e4m3").T @ gq
    Pi = mxq(f64(Ai), 0, "e4m3").T @ gq
    Pj = mxq(f64(Aj), 0, "e4m3").T @ gq
    Pk = mxq(f64(Ak), 0, "e4m3").T @ gq
    Pr_r, Pr_i, Pr_j, Pr_k = np.split(Pr, Q, axis=1)
    Pi_r, Pi_i, Pi_j, Pi_k = np.split(Pi, Q, axis=1)
    Pj_r, Pj_i, Pj_j, Pj_k = np.split(Pj, Q, axis=1)
    Pk_r, Pk_i, Pk_j, Pk_k = np.split(Pk, Q, axis=1)
    dx_r = Pr_r + Pi_i + Pj_j + Pk_k
    dx_i = Pr_i - Pi_r - Pj_k + Pk_j
    dx_j = Pr_j + Pi_k - Pj_r - Pk_i
    dx_k = Pr_k - Pi_j + Pj_i - Pk_r
    dx = np.concatenate([dx_r, dx_i, dx_j, dx_k], axis=1)
    dx = dx.reshape(N, C, T).transpose(1, 0, 2).reshape(B, C, N, T)
    dAr = mxq(g, 1, "e5m2") @ mxq(xn, 1, "e4m3").T
    return dx, dAr

@@ -1,0 +1,337 @@
+from contextlib import ExitStack
+
+import concourse.mybir as mybir
+from concourse.masks import make_identity
+
+C, N, T = 128, 1024, 8
+FLOPS = 5 * 2 * N * N * C * T
+
+F32 = mybir.dt.float32
+BF16 = mybir.dt.bfloat16
+I32 = mybir.dt.int32
+U8 = mybir.dt.uint8
+E4M3X4 = mybir.dt.float8_e4m3fn_x4
+E5M2X4 = mybir.dt.float8_e5m2_x4
+COPY = mybir.ActivationFunctionType.Copy
+
+P = 128
+PACK = 4
+HALF = 512
+GROUP = 32
+QSLOTS = 8
+MSLOTS = 6
+PIECE = 128
+EARLY_FIRST = (0, 1, 4, 5, 2, 3)
+EARLY = (0, 1, 2, 3, 4, 5)
+LATE = (6, 7)
+ORDER = ("r", "j", "k", "i")
+WINDOW = {"j": (0, 0), "r": (0, 2), "k": (1, 0), "i": (1, 2)}
+
+
+def tile_nconv_pa_v_kernel(tc, x, Ar, Ai, Aj, Ak, grad_out, out_0, out_1):
+    nc = tc.nc
+    adjacency = {"r": Ar, "i": Ai, "j": Aj, "k": Ak}
+    x_rows = x.rearrange("b c n t -> (b c) (n t)")
+    g_rows = grad_out.rearrange("b c n t -> (b c) (n t)")
+    dx_rows = out_0.rearrange("b c n t -> (b c) (n t)")
+
+    with ExitStack() as ctx:
+        keep = ctx.enter_context(tc.tile_pool(name="keep", bufs=1))
+        stream = ctx.enter_context(tc.tile_pool(name="stream", bufs=2))
+        psum = ctx.enter_context(tc.psum_pool(name="psum", bufs=1))
+        ctx.enter_context(tc.manual_schedule())
+
+        def bank(b):
+            return psum.tile([P, HALF], F32, name="bank%d" % b, tag="bank%d" % b)
+
+        ident = keep.tile([P, P], F32, name="ident")
+        make_identity(nc, ident[:])
+        sign = keep.tile([P, 1], F32, name="sign")
+        nc.gpsimd.memset(sign[:], 1.0)
+        nc.scalar.mul(sign[2 * GROUP : 3 * GROUP, :], sign[2 * GROUP : 3 * GROUP, :], -1.0)
+
+        signed = []
+        for w in range(2):
+            tile = keep.tile([P, PACK * QSLOTS * GROUP * PACK], BF16, name="signed%d" % w, align_bytes=64)
+            signed.append(tile)
+            pad = tile[:].bitcast(I32).rearrange("p (t s e) -> p t s e", t=PACK, s=QSLOTS)
+            nc.gpsimd.memset(pad[:, :, QSLOTS - 1, :], 0)
+        gn_codes, gn_scales = {}, {}
+        for h in range(2):
+            for chain, slots in enumerate((QSLOTS, MSLOTS)):
+                gn_codes[h, chain] = keep.tile([P, T * slots * GROUP], I32, name="gnc%d%d" % (h, chain), align_bytes=64)
+                gn_scales[h, chain] = keep.tile([P, T * slots * GROUP], U8, name="gns%d%d" % (h, chain), align_bytes=64)
+            nc.gpsimd.memset(gn_scales[h, 0][:].bitcast(I32), 0)
+
+        def load_twice(rows, u, h):
+            raw = stream.tile([P, HALF * T], BF16, name="raw", tag="raw", bufs=3)
+            src = rows[64 * u : 64 * (u + 1), :]
+            a, b = h * HALF * T, (h + 1) * HALF * T
+            nc.sync.dma_start(out=raw[0:P:2, :], in_=src[:, a:b])
+            nc.sync.dma_start(out=raw[1:P:2, 0 : HALF * T - PACK], in_=src[:, a + PACK : b])
+            return raw
+
+        def word_copy(engine, out, in_):
+            if engine == "scalar":
+                nc.scalar.copy(out=out, in_=in_)
+            else:
+                nc.vector.tensor_copy(out=out, in_=in_)
+
+        def compact_g(engine, raw, u, h):
+            gc = keep.tile([P, HALF * PACK], BF16, name="gc%d%d" % (u, h), align_bytes=64)
+            word_copy(
+                engine,
+                gc[:].bitcast(F32).rearrange("p (j q w) -> p j q w", j=PACK, w=2),
+                raw[:].bitcast(F32).rearrange("p (q j w) -> p j q w", j=PACK, w=4)[:, :, :, 0:2],
+            )
+            return gc
+
+        def compact_x(engine, raw):
+            xc = stream.tile([P, HALF * PACK], BF16, name="xc", tag="xc", bufs=2, align_bytes=64)
+            word_copy(
+                engine,
+                xc[:].bitcast(F32).rearrange("p (m w) -> p m w", w=2),
+                raw[:].bitcast(F32).rearrange("p (m w) -> p m w", w=4)[:, :, 0:2],
+            )
+            return xc
+
+        def quantize_keep(values, fmt, name):
+            codes = keep.tile([P, HALF], I32, name=name + "c", align_bytes=64)
+            scales = keep.tile([P, HALF], U8, name=name + "s", align_bytes=64)
+            nc.vector.quantize_mx(out=codes[:].bitcast(fmt), scales=scales[:], in_=values[:])
+            return codes, scales
+
+        def transpose_g(gc, w, b):
+            words = gc[:].bitcast(F32)
+            flipped = bank(b)
+            for j in range(PACK):
+                nc.tensor.transpose(flipped[:, j * P : (j + 1) * P], words[:, 2 * P * j + w : 2 * P * (j + 1) : 2], ident[:])
+            return flipped
+
+        def fill_signed(flipped, u, w):
+            slots = signed[w][:].rearrange("p (t s c j) -> p t s c j", t=PACK, s=QSLOTS, j=PACK)
+            into = slots[:, :, 2:4, :, :] if u == 0 else slots[:, :, 0:6:5, :, :]
+            nc.scalar.copy(out=into, in_=flipped[:].bitcast(BF16).rearrange("p (j s c t) -> p t s c j", j=PACK, s=2, t=PACK))
+
+        def negate(w):
+            slots = signed[w][:].rearrange("p (t s e) -> p t s e", t=PACK, s=QSLOTS)
+            nc.vector.tensor_scalar_mul(slots[:, :, 4:7:2, :], slots[:, :, 0:3:2, :], -1.0)
+            nc.vector.tensor_scalar_mul(slots[:, :, 1, :], slots[:, :, 5, :], -1.0)
+
+        def quantize_signed(h, w):
+            width = PACK * QSLOTS * GROUP
+            cols = slice(w * width, (w + 1) * width)
+            nc.vector.quantize_mx(out=gn_codes[h, 0][:, cols].bitcast(E5M2X4), scales=gn_scales[h, 0][:, cols], in_=signed[w][:])
+
+        def move_slots(h):
+            for src, dst in ((gn_codes[h, 0][:], gn_codes[h, 1][:]), (gn_scales[h, 0][:].bitcast(I32), gn_scales[h, 1][:].bitcast(I32))):
+                s = src.rearrange("p (t s e) -> p t s e", t=T, s=QSLOTS)
+                d = dst.rearrange("p (t a b e) -> p t a b e", t=T, a=2, b=3)
+                s6 = s[:, :, 0:6, :].rearrange("p t (b a) e -> p t a b e", a=3)
+                nc.vector.tensor_copy(out=d[:, :, :, 1:3, :], in_=s6[:, :, 0:2, :, :])
+                nc.vector.tensor_copy(out=d[:, :, :, 0, :], in_=s[:, :, 5:7, :])
+
+        def load_a(part, h, mh):
+            raw = stream.tile([P, PACK, HALF], BF16, name="araw", tag="araw", bufs=6)
+            rows = adjacency[part][h * HALF : (h + 1) * HALF, mh * HALF : (mh + 1) * HALF]
+            nc.sync.dma_start(out=raw[:], in_=rows.rearrange("(p j) m -> p j m", j=PACK))
+            return raw
+
+        def interleave_a(engine, raw):
+            grouped = stream.tile([P, HALF * PACK], BF16, name="agrp", tag="agrp", bufs=3, align_bytes=64)
+            word_copy(
+                engine,
+                grouped[:].rearrange("p (c i j) -> p c j i", i=4, j=PACK),
+                raw[:].rearrange("p j (c i) -> p c j i", i=4),
+            )
+            return grouped
+
+        def quantize_a(grouped):
+            codes = stream.tile([P, HALF], I32, name="acode", tag="acode", bufs=10, align_bytes=64)
+            scales = stream.tile([P, HALF], U8, name="ascale", tag="ascale", bufs=10, align_bytes=64)
+            nc.vector.quantize_mx(out=codes[:].bitcast(E4M3X4), scales=scales[:], in_=grouped[:])
+            return codes, scales
+
+        def dx_pass(acc, t, part, h, a_q, start, stop):
+            chain, slot = WINDOW[part]
+            place = PACK * ((t // 2) % 2) + 2 * (t // PACK) + t % 2
+            first = (place * (QSLOTS, MSLOTS)[chain] + slot) * GROUP
+            cols = slice(first, first + P)
+            nc.tensor.matmul_mx(
+                out=acc[:],
+                lhsT=gn_codes[h, chain][:, cols].bitcast(E5M2X4),
+                lhsT_scale=gn_scales[h, chain][:, cols],
+                rhs=a_q[0][:].bitcast(E4M3X4),
+                rhs_scale=a_q[1][:],
+                start=start,
+                stop=stop,
+            )
+
+        def empty_dx(acc, staged, tl):
+            nc.scalar.activation(out=staged[:, tl, :], in_=acc[:], func=COPY, scale=sign[:])
+
+        def weave_dx(engine, staged, piece, th, q):
+            word_copy(engine, piece[:, :, PACK * th : PACK * (th + 1)], staged[:, :, q * PIECE : (q + 1) * PIECE].rearrange("p t m -> p m t"))
+
+        def new_staged():
+            return stream.tile([P, PACK, HALF], F32, name="staged", tag="staged", bufs=2)
+
+        def new_pieces():
+            return [stream.tile([P, PIECE, T], F32, name="dxp", tag="dxp", bufs=4) for q in range(HALF // PIECE)]
+
+        def store_dx(piece, mh, q):
+            first = (mh * HALF + q * PIECE) * T
+            nc.sync.dma_start(out=dx_rows[:, first : first + PIECE * T], in_=piece[:].rearrange("p m t -> p (m t)"))
+
+        V, S = "vector", "scalar"
+        gc, grouped, a_q, accs = {}, {}, {}, {}
+        chunks = [(part, h) for h in range(2) for part in ORDER]
+
+        def passes(ts, s, last):
+            for t in ts:
+                dx_pass(accs[t], t, chunks[s][0], chunks[s][1], a_q[s], s == 0, s == last)
+
+        raw_g = [load_twice(g_rows, u, 0) for u in range(2)]
+        raw_a = [load_a(part, h, 0) for part, h in chunks[:2]]
+        for u in range(2):
+            gc[u, 0] = compact_g(V, raw_g[u], u, 0)
+            for w in range(2):
+                fill_signed(transpose_g(gc[u, 0], w, 4 + 2 * u + w), u, w)
+        raw_g = [load_twice(g_rows, u, 1) for u in range(2)]
+        raw_a.extend([load_a(part, h, 0) for part, h in chunks[2:6]])
+        grouped[0] = interleave_a(V, raw_a[0])
+        negate(0)
+        a_q[0] = quantize_a(grouped[0])
+        grouped[1] = interleave_a(S, raw_a[1])
+        raw_a.extend([load_a(part, h, 0) for part, h in chunks[6:8]])
+        quantize_signed(0, 0)
+        negate(1)
+        gc[0, 1] = compact_g(V, raw_g[0], 0, 1)
+        quantize_signed(0, 1)
+        gc[1, 1] = compact_g(S, raw_g[1], 1, 1)
+        a_q[1] = quantize_a(grouped[1])
+        for t in EARLY_FIRST:
+            accs[t] = bank(t)
+        passes(EARLY_FIRST[:4], 0, 7)
+        for w in range(2):
+            fill_signed(transpose_g(gc[0, 1], w, 6 + w), 0, w)
+        passes(EARLY_FIRST[4:], 0, 7)
+        passes(EARLY_FIRST, 1, 7)
+        grouped[2] = interleave_a(V, raw_a[2])
+        move_slots(0)
+        a_q[2] = quantize_a(grouped[2])
+        grouped[3] = interleave_a(S, raw_a[3])
+        grouped[4] = interleave_a(V, raw_a[4])
+        for w in range(2):
+            fill_signed(transpose_g(gc[1, 1], w, 6 + w), 1, w)
+        passes(EARLY_FIRST, 2, 7)
+        a_q[3] = quantize_a(grouped[3])
+        negate(0)
+        a_q[4] = quantize_a(grouped[4])
+        quantize_signed(1, 0)
+        negate(1)
+        grouped[5] = interleave_a(S, raw_a[5])
+        quantize_signed(1, 1)
+        passes(EARLY_FIRST, 3, 7)
+        for t in LATE:
+            accs[t] = bank(t)
+            for s in range(4):
+                passes([t], s, 7)
+        a_q[5] = quantize_a(grouped[5])
+        grouped[7] = interleave_a(S, raw_a[7])
+        move_slots(1)
+        grouped[6] = interleave_a(V, raw_a[6])
+        a_q[7] = quantize_a(grouped[7])
+        a_q[6] = quantize_a(grouped[6])
+        x_q, g_q, raw_x, xc = {}, {}, {}, {}
+        raw_b = [load_a(part, h, 1) for part, h in chunks[:2]]
+        for u in range(2):
+            raw_x[u, 0] = load_twice(x_rows, u, 0)
+        raw_b.extend([load_a(part, h, 1) for part, h in chunks[2:4]])
+        raw_x[0, 1] = load_twice(x_rows, 0, 1)
+        raw_b.extend([load_a(part, h, 1) for part, h in chunks[4:6]])
+        grouped = {s: interleave_a(V, raw_b[s]) for s in range(2)}
+        for u in range(2):
+            xc[u, 0] = compact_x(S, raw_x[u, 0])
+        raw_x[1, 1] = load_twice(x_rows, 1, 1)
+        raw_b.extend([load_a(part, h, 1) for part, h in chunks[6:8]])
+        first_q = quantize_a(grouped[0])
+        passes(EARLY_FIRST[:4] + EARLY_FIRST[4:] + LATE, 4, 7)
+        passes(range(T), 5, 7)
+        staged = [new_staged(), new_staged()]
+        for t in range(T):
+            passes([t], 6, 7)
+            passes([t], 7, 7)
+            empty_dx(accs[t], staged[t // PACK], t % PACK)
+
+        a_q = {0: first_q}
+        accs = {t: bank(t) for t in range(T)}
+        pieces = new_pieces()
+        keys = [(u, h) for h in range(2) for u in range(2)]
+        a_q[1] = quantize_a(grouped[1])
+        passes(range(T), 0, 7)
+        for q in range(4):
+            weave_dx(S, staged[0], pieces[q], 0, q)
+        for s in (2, 3):
+            grouped[s] = interleave_a(V, raw_b[s])
+            x_q[s - 2, 0] = quantize_keep(xc[s - 2, 0], E4M3X4, "xq%d0" % (s - 2))
+            a_q[s] = quantize_a(grouped[s])
+            passes(range(T), s - 1, 7)
+        grouped[4] = interleave_a(S, raw_b[4])
+        xc[0, 1] = compact_x(S, raw_x[0, 1])
+        grouped[5] = interleave_a(V, raw_b[5])
+        a_q[4] = quantize_a(grouped[4])
+        grouped[7] = interleave_a(S, raw_b[7])
+        a_q[5] = quantize_a(grouped[5])
+        grouped[6] = interleave_a(V, raw_b[6])
+        x_q[0, 1] = quantize_keep(xc[0, 1], E4M3X4, "xq01")
+        a_q[6] = quantize_a(grouped[6])
+        a_q[7] = quantize_a(grouped[7])
+        for q in range(4):
+            weave_dx(S, staged[1], pieces[q], 1, q)
+            store_dx(pieces[q], 0, q)
+        xc[1, 1] = compact_x(S, raw_x[1, 1])
+        for key in keys[:2]:
+            g_q[key] = quantize_keep(gc[key], E5M2X4, "gq%d%d" % key)
+        x_q[1, 1] = quantize_keep(xc[1, 1], E4M3X4, "xq11")
+        for key in keys[2:]:
+            g_q[key] = quantize_keep(gc[key], E5M2X4, "gq%d%d" % key)
+        for s in (3, 4, 5):
+            passes(range(T), s, 7)
+
+        def dar_step(step, engines):
+            nh, j = step // 4, step % 4
+            cols = slice(j * P, (j + 1) * P)
+            result = stream.tile([P, N], F32, name="dar", tag="dar", bufs=5)
+            for mh in range(2):
+                acc = bank((2 * step + mh) % 8)
+                for u in range(2):
+                    nc.tensor.matmul_mx(
+                        out=acc[:],
+                        lhsT=g_q[u, nh][0][:, cols].bitcast(E5M2X4),
+                        lhsT_scale=g_q[u, nh][1][:, cols],
+                        rhs=x_q[u, mh][0][:].bitcast(E4M3X4),
+                        rhs_scale=x_q[u, mh][1][:],
+                        start=(u == 0),
+                        stop=(u == 1),
+                    )
+                word_copy(engines[mh], result[:, mh * HALF : (mh + 1) * HALF], acc[:])
+            rows = out_1[nh * HALF : (nh + 1) * HALF, :].rearrange("(p j) m -> p j m", j=PACK)
+            nc.sync.dma_start(out=rows[:, j, :], in_=result[:])
+
+        staged = [new_staged(), new_staged()]
+        pieces = new_pieces()
+        for t in range(T):
+            passes([t], 6, 7)
+            passes([t], 7, 7)
+            empty_dx(accs[t], staged[t // PACK], t % PACK)
+            if t in (3, 5):
+                dar_step((t - 3) // 2, (V, V))
+            if t in (4, 6):
+                for q in (t - 4, t - 3):
+                    weave_dx(V, staged[0], pieces[q], 0, q)
+        for q in range(4):
+            weave_dx(V, staged[1], pieces[q], 1, q)
+            store_dx(pieces[q], 1, q)
+        for step in range(2, 8):
+            dar_step(step, (S, S if step < 4 else V))

@@ -24,6 +24,7 @@ PIECE = 128
 EARLY_FIRST = (0, 1, 4, 5, 2, 3)
 EARLY = (0, 1, 2, 3, 4, 5)
 LATE = (6, 7)
+BANK_OF = (0, 1, 4, 5, 2, 3, 6, 7)
 ORDER = ("r", "j", "k", "i")
 WINDOW = {"j": (0, 0), "r": (0, 2), "k": (1, 0), "i": (1, 2)}
 
@@ -113,15 +114,30 @@ def tile_nconv_pa_v_kernel(tc, x, Ar, Ai, Aj, Ak, grad_out, out_0, out_1):
             into = slots[:, :, 2:4, :, :] if u == 0 else slots[:, :, 0:6:5, :, :]
             nc.scalar.copy(out=into, in_=flipped[:].bitcast(BF16).rearrange("p (j s c t) -> p t s c j", j=PACK, s=2, t=PACK))
 
-        def negate(w):
-            slots = signed[w][:].rearrange("p (t s e) -> p t s e", t=PACK, s=QSLOTS)
+        def transpose_first(raw, pair, b):
+            words = raw[:].bitcast(F32)
+            flipped = bank(b)
+            for j in range(PACK):
+                nc.tensor.transpose(flipped[:, j * P : (j + 1) * P], words[:, PACK * j + pair : HALF * PACK : PACK * PACK], ident[:])
+            w, th = pair % 2, pair // 2
+            slots = signed[w][:].rearrange("p (t s c j) -> p t s c j", t=PACK, s=QSLOTS, j=PACK)[:, 2 * th : 2 * th + 2, :, :, :]
+            parts = flipped[:].bitcast(BF16).rearrange("p (j s c t) -> p t s c j", j=PACK, s=PACK, t=2)
+            nc.scalar.copy(out=slots[:, :, 0:6:5, :, :], in_=parts[:, :, 2:4, :, :])
+            nc.scalar.copy(out=slots[:, :, 2:4, :, :], in_=parts[:, :, 0:2, :, :])
+
+        def negate(w, lo=0, hi=PACK):
+            slots = signed[w][:].rearrange("p (t s e) -> p t s e", t=PACK, s=QSLOTS)[:, lo:hi, :, :]
             nc.vector.tensor_scalar_mul(slots[:, :, 4:7:2, :], slots[:, :, 0:3:2, :], -1.0)
             nc.vector.tensor_scalar_mul(slots[:, :, 1, :], slots[:, :, 5, :], -1.0)
 
-        def quantize_signed(h, w):
-            width = PACK * QSLOTS * GROUP
-            cols = slice(w * width, (w + 1) * width)
-            nc.vector.quantize_mx(out=gn_codes[h, 0][:, cols].bitcast(E5M2X4), scales=gn_scales[h, 0][:, cols], in_=signed[w][:])
+        def quantize_signed(h, w, lo=0, hi=PACK):
+            width = QSLOTS * GROUP
+            cols = slice((PACK * w + lo) * width, (PACK * w + hi) * width)
+            nc.vector.quantize_mx(
+                out=gn_codes[h, 0][:, cols].bitcast(E5M2X4),
+                scales=gn_scales[h, 0][:, cols],
+                in_=signed[w][:, lo * width * PACK : hi * width * PACK],
+            )
 
         def move_slots(h):
             for src, dst in ((gn_codes[h, 0][:], gn_codes[h, 1][:]), (gn_scales[h, 0][:].bitcast(I32), gn_scales[h, 1][:].bitcast(I32))):
@@ -191,58 +207,59 @@ def tile_nconv_pa_v_kernel(tc, x, Ar, Ai, Aj, Ak, grad_out, out_0, out_1):
             for t in ts:
                 dx_pass(accs[t], t, chunks[s][0], chunks[s][1], a_q[s], s == 0, s == last)
 
-        raw_g = [load_twice(g_rows, u, 0) for u in range(2)]
+        first_g = stream.tile([P, HALF * T], BF16, name="raw", tag="raw", bufs=3)
+        nc.sync.dma_start(out=first_g[:], in_=g_rows[:, 0 : HALF * T])
         raw_a = [load_a(part, h, 0) for part, h in chunks[:2]]
-        for u in range(2):
-            gc[u, 0] = compact_g(V, raw_g[u], u, 0)
-            for w in range(2):
-                fill_signed(transpose_g(gc[u, 0], w, 4 + 2 * u + w), u, w)
         raw_g = [load_twice(g_rows, u, 1) for u in range(2)]
         raw_a.extend([load_a(part, h, 0) for part, h in chunks[2:6]])
+        for pair, b in ((0, 6), (2, 7), (1, 4), (3, 5)):
+            transpose_first(first_g, pair, b)
         grouped[0] = interleave_a(V, raw_a[0])
-        negate(0)
+        negate(0, 0, 2)
         a_q[0] = quantize_a(grouped[0])
-        grouped[1] = interleave_a(S, raw_a[1])
+        quantize_signed(0, 0, 0, 2)
+        negate(0, 2, 4)
+        grouped[1] = interleave_a(V, raw_a[1])
         raw_a.extend([load_a(part, h, 0) for part, h in chunks[6:8]])
-        quantize_signed(0, 0)
+        quantize_signed(0, 0, 2, 4)
         negate(1)
-        gc[0, 1] = compact_g(V, raw_g[0], 0, 1)
-        quantize_signed(0, 1)
-        gc[1, 1] = compact_g(S, raw_g[1], 1, 1)
         a_q[1] = quantize_a(grouped[1])
+        quantize_signed(0, 1)
+        for u in range(2):
+            gc[u, 1] = compact_g(S, raw_g[u], u, 1)
         for t in EARLY_FIRST:
-            accs[t] = bank(t)
+            accs[t] = bank(BANK_OF[t])
         passes(EARLY_FIRST[:4], 0, 7)
         for w in range(2):
             fill_signed(transpose_g(gc[0, 1], w, 6 + w), 0, w)
-        passes(EARLY_FIRST[4:], 0, 7)
-        passes(EARLY_FIRST, 1, 7)
+        passes(EARLY_FIRST[:4], 1, 7)
+        for w in range(2):
+            fill_signed(transpose_g(gc[1, 1], w, 6 + w), 1, w)
+            passes(EARLY_FIRST[4:], w, 7)
         grouped[2] = interleave_a(V, raw_a[2])
         move_slots(0)
         a_q[2] = quantize_a(grouped[2])
-        grouped[3] = interleave_a(S, raw_a[3])
-        grouped[4] = interleave_a(V, raw_a[4])
-        for w in range(2):
-            fill_signed(transpose_g(gc[1, 1], w, 6 + w), 1, w)
-        passes(EARLY_FIRST, 2, 7)
-        a_q[3] = quantize_a(grouped[3])
+        grouped[3] = interleave_a(V, raw_a[3])
         negate(0)
-        a_q[4] = quantize_a(grouped[4])
+        a_q[3] = quantize_a(grouped[3])
+        grouped[4] = interleave_a(S, raw_a[4])
         quantize_signed(1, 0)
         negate(1)
+        a_q[4] = quantize_a(grouped[4])
         grouped[5] = interleave_a(S, raw_a[5])
         quantize_signed(1, 1)
-        passes(EARLY_FIRST, 3, 7)
+        passes(EARLY_FIRST, 2, 7)
         for t in LATE:
-            accs[t] = bank(t)
-            for s in range(4):
+            accs[t] = bank(BANK_OF[t])
+            for s in range(3):
                 passes([t], s, 7)
+        passes(range(T), 3, 7)
+        grouped[6] = interleave_a(V, raw_a[6])
         a_q[5] = quantize_a(grouped[5])
         grouped[7] = interleave_a(S, raw_a[7])
         move_slots(1)
-        grouped[6] = interleave_a(V, raw_a[6])
-        a_q[7] = quantize_a(grouped[7])
         a_q[6] = quantize_a(grouped[6])
+        a_q[7] = quantize_a(grouped[7])
         x_q, g_q, raw_x, xc = {}, {}, {}, {}
         raw_b = [load_a(part, h, 1) for part, h in chunks[:2]]
         for u in range(2):
@@ -255,6 +272,7 @@ def tile_nconv_pa_v_kernel(tc, x, Ar, Ai, Aj, Ak, grad_out, out_0, out_1):
             xc[u, 0] = compact_x(S, raw_x[u, 0])
         raw_x[1, 1] = load_twice(x_rows, 1, 1)
         raw_b.extend([load_a(part, h, 1) for part, h in chunks[6:8]])
+        raw_g = [load_twice(g_rows, 0, 0)]
         first_q = quantize_a(grouped[0])
         passes(EARLY_FIRST[:4] + EARLY_FIRST[4:] + LATE, 4, 7)
         passes(range(T), 5, 7)
@@ -265,7 +283,7 @@ def tile_nconv_pa_v_kernel(tc, x, Ar, Ai, Aj, Ak, grad_out, out_0, out_1):
             empty_dx(accs[t], staged[t // PACK], t % PACK)
 
         a_q = {0: first_q}
-        accs = {t: bank(t) for t in range(T)}
+        accs = {t: bank(BANK_OF[t]) for t in range(T)}
         pieces = new_pieces()
         keys = [(u, h) for h in range(2) for u in range(2)]
         a_q[1] = quantize_a(grouped[1])
@@ -279,6 +297,7 @@ def tile_nconv_pa_v_kernel(tc, x, Ar, Ai, Aj, Ak, grad_out, out_0, out_1):
             passes(range(T), s - 1, 7)
         grouped[4] = interleave_a(S, raw_b[4])
         xc[0, 1] = compact_x(S, raw_x[0, 1])
+        raw_g.append(load_twice(g_rows, 1, 0))
         grouped[5] = interleave_a(V, raw_b[5])
         a_q[4] = quantize_a(grouped[4])
         grouped[7] = interleave_a(S, raw_b[7])
@@ -291,20 +310,22 @@ def tile_nconv_pa_v_kernel(tc, x, Ar, Ai, Aj, Ak, grad_out, out_0, out_1):
             weave_dx(S, staged[1], pieces[q], 1, q)
             store_dx(pieces[q], 0, q)
         xc[1, 1] = compact_x(S, raw_x[1, 1])
-        for key in keys[:2]:
-            g_q[key] = quantize_keep(gc[key], E5M2X4, "gq%d%d" % key)
-        x_q[1, 1] = quantize_keep(xc[1, 1], E4M3X4, "xq11")
         for key in keys[2:]:
+            g_q[key] = quantize_keep(gc[key], E5M2X4, "gq%d%d" % key)
+        for u in range(2):
+            gc[u, 0] = compact_g(V, raw_g[u], u, 0)
+        x_q[1, 1] = quantize_keep(xc[1, 1], E4M3X4, "xq11")
+        for key in keys[:2]:
             g_q[key] = quantize_keep(gc[key], E5M2X4, "gq%d%d" % key)
         for s in (3, 4, 5):
             passes(range(T), s, 7)
 
         def dar_step(step, engines):
-            nh, j = step // 4, step % 4
+            nh, j = 1 - step // 4, step % 4
             cols = slice(j * P, (j + 1) * P)
             result = stream.tile([P, N], F32, name="dar", tag="dar", bufs=5)
             for mh in range(2):
-                acc = bank((2 * step + mh) % 8)
+                acc = bank(BANK_OF[(2 * step + mh) % 8])
                 for u in range(2):
                     nc.tensor.matmul_mx(
                         out=acc[:],

from contextlib import ExitStack

import concourse.mybir as mybir
from concourse.masks import make_identity

C, N, T = 128, 1024, 8
FLOPS = 5 * 2 * N * N * C * T

F32 = mybir.dt.float32
BF16 = mybir.dt.bfloat16
I32 = mybir.dt.int32
U8 = mybir.dt.uint8
E4M3X4 = mybir.dt.float8_e4m3fn_x4
E5M2X4 = mybir.dt.float8_e5m2_x4
COPY = mybir.ActivationFunctionType.Copy

P = 128
PACK = 4
HALF = 512
GROUP = 32
QSLOTS = 8
MSLOTS = 6
PIECE = 128
EARLY_FIRST = (0, 1, 4, 5, 2, 3)
EARLY = (0, 1, 2, 3, 4, 5)
LATE = (6, 7)
BANK_OF = (0, 1, 4, 5, 2, 3, 6, 7)
ORDER = ("r", "j", "k", "i")
WINDOW = {"j": (0, 0), "r": (0, 2), "k": (1, 0), "i": (1, 2)}


def tile_nconv_pa_v_kernel(tc, x, Ar, Ai, Aj, Ak, grad_out, out_0, out_1):
    nc = tc.nc
    adjacency = {"r": Ar, "i": Ai, "j": Aj, "k": Ak}
    x_rows = x.rearrange("b c n t -> (b c) (n t)")
    g_rows = grad_out.rearrange("b c n t -> (b c) (n t)")
    dx_rows = out_0.rearrange("b c n t -> (b c) (n t)")

    with ExitStack() as ctx:
        keep = ctx.enter_context(tc.tile_pool(name="keep", bufs=1))
        stream = ctx.enter_context(tc.tile_pool(name="stream", bufs=2))
        psum = ctx.enter_context(tc.psum_pool(name="psum", bufs=1))
        ctx.enter_context(tc.manual_schedule())

        def bank(b):
            return psum.tile([P, HALF], F32, name="bank%d" % b, tag="bank%d" % b)

        ident = keep.tile([P, P], F32, name="ident")
        make_identity(nc, ident[:])
        sign = keep.tile([P, 1], F32, name="sign")
        nc.gpsimd.memset(sign[:], 1.0)
        nc.scalar.mul(sign[2 * GROUP : 3 * GROUP, :], sign[2 * GROUP : 3 * GROUP, :], -1.0)

        signed = []
        for w in range(2):
            tile = keep.tile([P, PACK * QSLOTS * GROUP * PACK], BF16, name="signed%d" % w, align_bytes=64)
            signed.append(tile)
            pad = tile[:].bitcast(I32).rearrange("p (t s e) -> p t s e", t=PACK, s=QSLOTS)
            nc.gpsimd.memset(pad[:, :, QSLOTS - 1, :], 0)
        gn_codes, gn_scales = {}, {}
        for h in range(2):
            for chain, slots in enumerate((QSLOTS, MSLOTS)):
                gn_codes[h, chain] = keep.tile([P, T * slots * GROUP], I32, name="gnc%d%d" % (h, chain), align_bytes=64)
                gn_scales[h, chain] = keep.tile([P, T * slots * GROUP], U8, name="gns%d%d" % (h, chain), align_bytes=64)
            nc.gpsimd.memset(gn_scales[h, 0][:].bitcast(I32), 0)

        def load_twice(rows, u, h):
            raw = stream.tile([P, HALF * T], BF16, name="raw", tag="raw", bufs=3)
            src = rows[64 * u : 64 * (u + 1), :]
            a, b = h * HALF * T, (h + 1) * HALF * T
            nc.sync.dma_start(out=raw[0:P:2, :], in_=src[:, a:b])
            nc.sync.dma_start(out=raw[1:P:2, 0 : HALF * T - PACK], in_=src[:, a + PACK : b])
            return raw

        def word_copy(engine, out, in_):
            if engine == "scalar":
                nc.scalar.copy(out=out, in_=in_)
            else:
                nc.vector.tensor_copy(out=out, in_=in_)

        def compact_g(engine, raw, u, h):
            gc = keep.tile([P, HALF * PACK], BF16, name="gc%d%d" % (u, h), align_bytes=64)
            word_copy(
                engine,
                gc[:].bitcast(F32).rearrange("p (j q w) -> p j q w", j=PACK, w=2),
                raw[:].bitcast(F32).rearrange("p (q j w) -> p j q w", j=PACK, w=4)[:, :, :, 0:2],
            )
            return gc

        def compact_x(engine, raw):
            xc = stream.tile([P, HALF * PACK], BF16, name="xc", tag="xc", bufs=2, align_bytes=64)
            word_copy(
                engine,
                xc[:].bitcast(F32).rearrange("p (m w) -> p m w", w=2),
                raw[:].bitcast(F32).rearrange("p (m w) -> p m w", w=4)[:, :, 0:2],
            )
            return xc

        def quantize_keep(values, fmt, name):
            codes = keep.tile([P, HALF], I32, name=name + "c", align_bytes=64)
            scales = keep.tile([P, HALF], U8, name=name + "s", align_bytes=64)
            nc.vector.quantize_mx(out=codes[:].bitcast(fmt), scales=scales[:], in_=values[:])
            return codes, scales

        def transpose_g(gc, w, b):
            words = gc[:].bitcast(F32)
            flipped = bank(b)
            for j in range(PACK):
                nc.tensor.transpose(flipped[:, j * P : (j + 1) * P], words[:, 2 * P * j + w : 2 * P * (j + 1) : 2], ident[:])
            return flipped

        def fill_signed(flipped, u, w):
            slots = signed[w][:].rearrange("p (t s c j) -> p t s c j", t=PACK, s=QSLOTS, j=PACK)
            into = slots[:, :, 2:4, :, :] if u == 0 else slots[:, :, 0:6:5, :, :]
            nc.scalar.copy(out=into, in_=flipped[:].bitcast(BF16).rearrange("p (j s c t) -> p t s c j", j=PACK, s=2, t=PACK))

        def transpose_first(raw, pair, b):
            words = raw[:].bitcast(F32)
            flipped = bank(b)
            for j in range(PACK):
                nc.tensor.transpose(flipped[:, j * P : (j + 1) * P], words[:, PACK * j + pair : HALF * PACK : PACK * PACK], ident[:])
            w, th = pair % 2, pair // 2
            slots = signed[w][:].rearrange("p (t s c j) -> p t s c j", t=PACK, s=QSLOTS, j=PACK)[:, 2 * th : 2 * th + 2, :, :, :]
            parts = flipped[:].bitcast(BF16).rearrange("p (j s c t) -> p t s c j", j=PACK, s=PACK, t=2)
            nc.scalar.copy(out=slots[:, :, 0:6:5, :, :], in_=parts[:, :, 2:4, :, :])
            nc.scalar.copy(out=slots[:, :, 2:4, :, :], in_=parts[:, :, 0:2, :, :])

        def negate(w, lo=0, hi=PACK):
            slots = signed[w][:].rearrange("p (t s e) -> p t s e", t=PACK, s=QSLOTS)[:, lo:hi, :, :]
            nc.vector.tensor_scalar_mul(slots[:, :, 4:7:2, :], slots[:, :, 0:3:2, :], -1.0)
            nc.vector.tensor_scalar_mul(slots[:, :, 1, :], slots[:, :, 5, :], -1.0)

        def quantize_signed(h, w, lo=0, hi=PACK):
            width = QSLOTS * GROUP
            cols = slice((PACK * w + lo) * width, (PACK * w + hi) * width)
            nc.vector.quantize_mx(
                out=gn_codes[h, 0][:, cols].bitcast(E5M2X4),
                scales=gn_scales[h, 0][:, cols],
                in_=signed[w][:, lo * width * PACK : hi * width * PACK],
            )

        def move_slots(h):
            for src, dst in ((gn_codes[h, 0][:], gn_codes[h, 1][:]), (gn_scales[h, 0][:].bitcast(I32), gn_scales[h, 1][:].bitcast(I32))):
                s = src.rearrange("p (t s e) -> p t s e", t=T, s=QSLOTS)
                d = dst.rearrange("p (t a b e) -> p t a b e", t=T, a=2, b=3)
                s6 = s[:, :, 0:6, :].rearrange("p t (b a) e -> p t a b e", a=3)
                nc.vector.tensor_copy(out=d[:, :, :, 1:3, :], in_=s6[:, :, 0:2, :, :])
                nc.vector.tensor_copy(out=d[:, :, :, 0, :], in_=s[:, :, 5:7, :])

        def load_a(part, h, mh):
            raw = stream.tile([P, PACK, HALF], BF16, name="araw", tag="araw", bufs=6)
            rows = adjacency[part][h * HALF : (h + 1) * HALF, mh * HALF : (mh + 1) * HALF]
            nc.sync.dma_start(out=raw[:], in_=rows.rearrange("(p j) m -> p j m", j=PACK))
            return raw

        def interleave_a(engine, raw):
            grouped = stream.tile([P, HALF * PACK], BF16, name="agrp", tag="agrp", bufs=3, align_bytes=64)
            word_copy(
                engine,
                grouped[:].rearrange("p (c i j) -> p c j i", i=4, j=PACK),
                raw[:].rearrange("p j (c i) -> p c j i", i=4),
            )
            return grouped

        def quantize_a(grouped):
            codes = stream.tile([P, HALF], I32, name="acode", tag="acode", bufs=10, align_bytes=64)
            scales = stream.tile([P, HALF], U8, name="ascale", tag="ascale", bufs=10, align_bytes=64)
            nc.vector.quantize_mx(out=codes[:].bitcast(E4M3X4), scales=scales[:], in_=grouped[:])
            return codes, scales

        def dx_pass(acc, t, part, h, a_q, start, stop):
            chain, slot = WINDOW[part]
            place = PACK * ((t // 2) % 2) + 2 * (t // PACK) + t % 2
            first = (place * (QSLOTS, MSLOTS)[chain] + slot) * GROUP
            cols = slice(first, first + P)
            nc.tensor.matmul_mx(
                out=acc[:],
                lhsT=gn_codes[h, chain][:, cols].bitcast(E5M2X4),
                lhsT_scale=gn_scales[h, chain][:, cols],
                rhs=a_q[0][:].bitcast(E4M3X4),
                rhs_scale=a_q[1][:],
                start=start,
                stop=stop,
            )

        def empty_dx(acc, staged, tl):
            nc.scalar.activation(out=staged[:, tl, :], in_=acc[:], func=COPY, scale=sign[:])

        def weave_dx(engine, staged, piece, th, q):
            word_copy(engine, piece[:, :, PACK * th : PACK * (th + 1)], staged[:, :, q * PIECE : (q + 1) * PIECE].rearrange("p t m -> p m t"))

        def new_staged():
            return stream.tile([P, PACK, HALF], F32, name="staged", tag="staged", bufs=2)

        def new_pieces():
            return [stream.tile([P, PIECE, T], F32, name="dxp", tag="dxp", bufs=4) for q in range(HALF // PIECE)]

        def store_dx(piece, mh, q):
            first = (mh * HALF + q * PIECE) * T
            nc.sync.dma_start(out=dx_rows[:, first : first + PIECE * T], in_=piece[:].rearrange("p m t -> p (m t)"))

        V, S = "vector", "scalar"
        gc, grouped, a_q, accs = {}, {}, {}, {}
        chunks = [(part, h) for h in range(2) for part in ORDER]

        def passes(ts, s, last):
            for t in ts:
                dx_pass(accs[t], t, chunks[s][0], chunks[s][1], a_q[s], s == 0, s == last)

        first_g = stream.tile([P, HALF * T], BF16, name="raw", tag="raw", bufs=3)
        nc.sync.dma_start(out=first_g[:], in_=g_rows[:, 0 : HALF * T])
        raw_a = [load_a(part, h, 0) for part, h in chunks[:2]]
        raw_g = [load_twice(g_rows, u, 1) for u in range(2)]
        raw_a.extend([load_a(part, h, 0) for part, h in chunks[2:6]])
        for pair, b in ((0, 6), (2, 7), (1, 4), (3, 5)):
            transpose_first(first_g, pair, b)
        grouped[0] = interleave_a(V, raw_a[0])
        negate(0, 0, 2)
        a_q[0] = quantize_a(grouped[0])
        quantize_signed(0, 0, 0, 2)
        negate(0, 2, 4)
        grouped[1] = interleave_a(V, raw_a[1])
        raw_a.extend([load_a(part, h, 0) for part, h in chunks[6:8]])
        quantize_signed(0, 0, 2, 4)
        negate(1)
        a_q[1] = quantize_a(grouped[1])
        quantize_signed(0, 1)
        for u in range(2):
            gc[u, 1] = compact_g(S, raw_g[u], u, 1)
        for t in EARLY_FIRST:
            accs[t] = bank(BANK_OF[t])
        passes(EARLY_FIRST[:4], 0, 7)
        for w in range(2):
            fill_signed(transpose_g(gc[0, 1], w, 6 + w), 0, w)
        passes(EARLY_FIRST[:4], 1, 7)
        for w in range(2):
            fill_signed(transpose_g(gc[1, 1], w, 6 + w), 1, w)
            passes(EARLY_FIRST[4:], w, 7)
        grouped[2] = interleave_a(V, raw_a[2])
        move_slots(0)
        a_q[2] = quantize_a(grouped[2])
        grouped[3] = interleave_a(V, raw_a[3])
        negate(0)
        a_q[3] = quantize_a(grouped[3])
        grouped[4] = interleave_a(S, raw_a[4])
        quantize_signed(1, 0)
        negate(1)
        a_q[4] = quantize_a(grouped[4])
        grouped[5] = interleave_a(S, raw_a[5])
        quantize_signed(1, 1)
        passes(EARLY_FIRST, 2, 7)
        for t in LATE:
            accs[t] = bank(BANK_OF[t])
            for s in range(3):
                passes([t], s, 7)
        passes(range(T), 3, 7)
        grouped[6] = interleave_a(V, raw_a[6])
        a_q[5] = quantize_a(grouped[5])
        grouped[7] = interleave_a(S, raw_a[7])
        move_slots(1)
        a_q[6] = quantize_a(grouped[6])
        a_q[7] = quantize_a(grouped[7])
        x_q, g_q, raw_x, xc = {}, {}, {}, {}
        raw_b = [load_a(part, h, 1) for part, h in chunks[:2]]
        for u in range(2):
            raw_x[u, 0] = load_twice(x_rows, u, 0)
        raw_b.extend([load_a(part, h, 1) for part, h in chunks[2:4]])
        raw_x[0, 1] = load_twice(x_rows, 0, 1)
        raw_b.extend([load_a(part, h, 1) for part, h in chunks[4:6]])
        grouped = {s: interleave_a(V, raw_b[s]) for s in range(2)}
        for u in range(2):
            xc[u, 0] = compact_x(S, raw_x[u, 0])
        raw_x[1, 1] = load_twice(x_rows, 1, 1)
        raw_b.extend([load_a(part, h, 1) for part, h in chunks[6:8]])
        raw_g = [load_twice(g_rows, 0, 0)]
        first_q = quantize_a(grouped[0])
        passes(EARLY_FIRST[:4] + EARLY_FIRST[4:] + LATE, 4, 7)
        passes(range(T), 5, 7)
        staged = [new_staged(), new_staged()]
        for t in range(T):
            passes([t], 6, 7)
            passes([t], 7, 7)
            empty_dx(accs[t], staged[t // PACK], t % PACK)

        a_q = {0: first_q}
        accs = {t: bank(BANK_OF[t]) for t in range(T)}
        pieces = new_pieces()
        keys = [(u, h) for h in range(2) for u in range(2)]
        a_q[1] = quantize_a(grouped[1])
        passes(range(T), 0, 7)
        for q in range(4):
            weave_dx(S, staged[0], pieces[q], 0, q)
        for s in (2, 3):
            grouped[s] = interleave_a(V, raw_b[s])
            x_q[s - 2, 0] = quantize_keep(xc[s - 2, 0], E4M3X4, "xq%d0" % (s - 2))
            a_q[s] = quantize_a(grouped[s])
            passes(range(T), s - 1, 7)
        grouped[4] = interleave_a(S, raw_b[4])
        xc[0, 1] = compact_x(S, raw_x[0, 1])
        raw_g.append(load_twice(g_rows, 1, 0))
        grouped[5] = interleave_a(V, raw_b[5])
        a_q[4] = quantize_a(grouped[4])
        grouped[7] = interleave_a(S, raw_b[7])
        a_q[5] = quantize_a(grouped[5])
        grouped[6] = interleave_a(V, raw_b[6])
        x_q[0, 1] = quantize_keep(xc[0, 1], E4M3X4, "xq01")
        a_q[6] = quantize_a(grouped[6])
        a_q[7] = quantize_a(grouped[7])
        for q in range(4):
            weave_dx(S, staged[1], pieces[q], 1, q)
            store_dx(pieces[q], 0, q)
        xc[1, 1] = compact_x(S, raw_x[1, 1])
        for key in keys[2:]:
            g_q[key] = quantize_keep(gc[key], E5M2X4, "gq%d%d" % key)
        for u in range(2):
            gc[u, 0] = compact_g(V, raw_g[u], u, 0)
        x_q[1, 1] = quantize_keep(xc[1, 1], E4M3X4, "xq11")
        for key in keys[:2]:
            g_q[key] = quantize_keep(gc[key], E5M2X4, "gq%d%d" % key)
        for s in (3, 4, 5):
            passes(range(T), s, 7)

        def dar_step(step, engines):
            nh, j = 1 - step // 4, step % 4
            cols = slice(j * P, (j + 1) * P)
            result = stream.tile([P, N], F32, name="dar", tag="dar", bufs=5)
            for mh in range(2):
                acc = bank(BANK_OF[(2 * step + mh) % 8])
                for u in range(2):
                    nc.tensor.matmul_mx(
                        out=acc[:],
                        lhsT=g_q[u, nh][0][:, cols].bitcast(E5M2X4),
                        lhsT_scale=g_q[u, nh][1][:, cols],
                        rhs=x_q[u, mh][0][:].bitcast(E4M3X4),
                        rhs_scale=x_q[u, mh][1][:],
                        start=(u == 0),
                        stop=(u == 1),
                    )
                word_copy(engines[mh], result[:, mh * HALF : (mh + 1) * HALF], acc[:])
            rows = out_1[nh * HALF : (nh + 1) * HALF, :].rearrange("(p j) m -> p j m", j=PACK)
            nc.sync.dma_start(out=rows[:, j, :], in_=result[:])

        staged = [new_staged(), new_staged()]
        pieces = new_pieces()
        for t in range(T):
            passes([t], 6, 7)
            passes([t], 7, 7)
            empty_dx(accs[t], staged[t // PACK], t % PACK)
            if t in (3, 5):
                dar_step((t - 3) // 2, (V, V))
            if t in (4, 6):
                for q in (t - 4, t - 3):
                    weave_dx(V, staged[0], pieces[q], 0, q)
        for q in range(4):
            weave_dx(V, staged[1], pieces[q], 1, q)
            store_dx(pieces[q], 1, q)
        for step in range(2, 8):
            dar_step(step, (S, S if step < 4 else V))
